import numpy as np
import ml_dtypes


def mxq(x, axis, fmt="e4m3"):
    dtype, down = {"e4m3": (ml_dtypes.float8_e4m3fn, 7), "e5m2": (ml_dtypes.float8_e5m2, 14)}[fmt]
    v = np.moveaxis(np.asarray(x, np.float32).astype(ml_dtypes.bfloat16).astype(np.float64), axis, -1)
    blocks = v.reshape(v.shape[:-1] + (-1, 32))
    amax = np.abs(blocks).max(-1, keepdims=True)
    byte = np.maximum(np.where(amax > 0, np.frexp(amax)[1] - 1 + 127, 0) - down, 1)
    scale = np.exp2(byte - 127.0)
    codes = (blocks / scale).astype(np.float32).astype(dtype).astype(np.float64)
    return np.moveaxis((codes * scale).reshape(v.shape), -1, axis)


WIDE = False


def mx_kscale(k):
    if not WIDE:
        return np.ones(k)
    levels = np.array([10, -10, 5, -5, 0])
    if k % 512:
        return np.exp2(np.random.permutation(np.resize(levels, k // 32))).repeat(32)
    a = np.empty((k // 512, 16))
    for p in range(k // 512):
        a[p, :8] = np.random.permutation(np.resize(levels, 8))
        for g in range(8):
            far = levels[np.abs(levels - a[p, g]) >= 10]
            a[p, g + 8] = far[np.random.randint(len(far))]
    return np.exp2(a.ravel()).repeat(32)


BF16 = ml_dtypes.bfloat16


def bf(x):
    return np.asarray(x, np.float32).astype(BF16)


def f64(x):
    return np.asarray(x).astype(np.float64)


E2M1 = np.array([0.0, 0.5, 1.0, 1.5, 2.0, 3.0, 4.0, 6.0, -0.0, -0.5, -1.0, -1.5, -2.0, -3.0, -4.0, -6.0])


def pack_weight(w, fmt):
    k, n = w.shape
    w = f64(bf(w)).reshape(k // 32, 32, n)
    amax = np.abs(w).max(1)
    if fmt == "e4m3":
        byte = np.frexp(amax)[1] - 1 + 127 - 7
    else:
        mant, ex = np.frexp(amax / 6.0)
        byte = np.where(mant > 0.5, ex, ex - 1) + 127
    byte = np.clip(np.where(amax > 0, byte, 1), 1, 254)
    scaled = (w * np.exp2(127.0 - byte)[:, None, :]).reshape(k, n).astype(np.float32)
    by_word = np.ascontiguousarray(scaled.reshape(k // 512, 128, 4, n).transpose(0, 1, 3, 2))
    if fmt == "e4m3":
        words = by_word.astype(ml_dtypes.float8_e4m3fn).view(np.uint8)
    else:
        c = by_word.astype(ml_dtypes.float4_e2m1fn).view(np.uint8) & 0xF
        words = c[..., 0::2] | (c[..., 1::2] << 4)
    return np.ascontiguousarray(words), np.ascontiguousarray(byte.astype(np.uint8).reshape(k // 512, 16, n))


def unpack_weight(words, scales, fmt):
    g, p, n, _ = words.shape
    if fmt == "e4m3":
        vals = np.ascontiguousarray(words).view(ml_dtypes.float8_e4m3fn).astype(np.float64)
    else:
        nib = np.empty((g, p, n, 4), np.uint8)
        nib[..., 0::2] = words & 0xF
        nib[..., 1::2] = words >> 4
        vals = E2M1[nib]
    vals = vals * np.repeat(np.exp2(scales.astype(np.float64) - 127.0), 8, axis=1)[..., None]
    return vals.transpose(0, 1, 3, 2).reshape(g * 512, n)


B, N, K, H, NUM_IN = 4, 64, 30, 512, 512


def draw0():
    s, t = mx_kscale(H), mx_kscale(H)
    u = np.random.standard_normal((B, N, H))
    e = np.random.standard_normal((B, N, K, H))
    h1 = bf(np.maximum((u[:, :, None, :] + e) * 0.7, 0.0) * s)
    h_V = bf(np.random.standard_normal((B, N, H)))
    mask_attend = bf(np.random.random((B, N, K)) < 0.9)
    W2_words, W2_scales = pack_weight(np.random.standard_normal((H, H)) * 1.4 / np.sqrt(H) / s[:, None] * t, "e4m3")
    b2 = bf(np.random.standard_normal(H) * 0.2 * t)
    W3_words, W3_scales = pack_weight(np.random.standard_normal((H, H)) * 2.8 / np.sqrt(H) / t[:, None], "e4m3")
    b3 = bf(np.random.standard_normal(H) * 0.2)
    return {"h1": h1,
            "h_V": h_V,
            "mask_attend": mask_attend,
            "W2_words": W2_words,
            "W2_scales": W2_scales,
            "b2": b2,
            "W3_words": W3_words,
            "W3_scales": W3_scales,
            "b3": b3}


def core(h1, h_V, mask_attend, W2_words, W2_scales, b2, W3_words, W3_scales, b3):
    h2 = np.maximum((mxq(f64(h1), 3, "e4m3") @ unpack_weight(W2_words, W2_scales, "e4m3")) + f64(b2), 0.0)
    msg = ((mxq(h2, 3, "e4m3") @ unpack_weight(W3_words, W3_scales, "e4m3")) + f64(b3)) * f64(mask_attend)[..., None]
    return f64(h_V) + np.mean(msg, axis=-2)


def e4m3fn_bytes(y):
    return np.clip(np.asarray(y, np.float64), -448.0, 448.0).astype(np.float32).astype(ml_dtypes.float8_e4m3fn).view(np.uint8)


def e4m3fn_values(b):
    return np.asarray(b, np.uint8).view(ml_dtypes.float8_e4m3fn).astype(np.float64)


def setup_inputs():
    d = draw0()
    x0 = np.asarray(d['h1']).astype(np.float64)
    s = (np.max(np.abs(x0), axis=(0, 1, 2), keepdims=True) / 448.0).astype(np.float32)
    out = {}
    for k, v in d.items():
        if k == 'h1':
            out['h1_bytes'] = e4m3fn_bytes(x0 / s.astype(np.float64))
            out['h1_scale'] = s
        else:
            out[k] = v
    return out


def reference(h1_bytes, h1_scale, h_V, mask_attend, W2_words, W2_scales, b2, W3_words, W3_scales, b3):
    return core(e4m3fn_values(h1_bytes) * h1_scale.astype(np.float64), h_V, mask_attend, W2_words, W2_scales, b2, W3_words, W3_scales, b3)

@@ -1,0 +1,315 @@
+from contextlib import ExitStack
+
+import concourse.mybir as mybir
+from concourse.masks import make_identity
+
+P = 128
+NODES = 256
+NEIGHBOURS = 30
+H = 512
+PACK = 4
+NODE_BLOCKS = NODES // P
+GROUPS = NODE_BLOCKS * NEIGHBOURS
+UNIT = 4
+UNITS = GROUPS // UNIT
+TOK = UNIT * P
+FLOPS = 2 * (2 * NODES * NEIGHBOURS * H * H)
+
+F32 = mybir.dt.float32
+BF16 = mybir.dt.bfloat16
+I32 = mybir.dt.int32
+U8 = mybir.dt.uint8
+FP8 = mybir.dt.float8_e4m3fn
+FP8X4 = mybir.dt.float8_e4m3fn_x4
+ALU = mybir.AluOpType
+ACT = mybir.ActivationFunctionType
+AXIS = mybir.AxisListType
+
+CAST_ON_SCALAR = (3,)
+
+
+def tile_mpnnlayer_pb_w8_kernel(
+    tc, h1_bytes, h1_scale, h_V, mask_attend, W2_words, W2_scales, b2, W3_words, W3_scales, b3, out
+):
+    nc = tc.nc
+    bytes_rows = h1_bytes.rearrange("b n j k -> (b n) (j k)")
+    out_rows = out.rearrange("b n h -> (b n) h")
+
+    with ExitStack() as ctx:
+        ctx.enter_context(tc.manual_schedule())
+        keep = ctx.enter_context(tc.tile_pool(name="keep", bufs=1))
+        work = ctx.enter_context(tc.tile_pool(name="work", bufs=2))
+        psum = ctx.enter_context(tc.psum_pool(name="psum", bufs=1))
+
+        h1b = keep.tile([P, NODE_BLOCKS, NEIGHBOURS * H], U8, name="h1b", align_bytes=64)
+        mask_bf = keep.tile([P, NODE_BLOCKS, NEIGHBOURS], BF16, name="mask_bf")
+        mask_f = keep.tile([P, GROUPS], F32, name="mask_f")
+        k_scale = keep.tile([P, PACK], F32, name="k_scale")
+        bias_bf = keep.tile([P, PACK], BF16, name="bias_bf")
+        bias_f = keep.tile([P, PACK], F32, name="bias_f")
+        ident = keep.tile([P, P], F32, name="ident")
+        w2_raw = keep.tile([P, H], I32, name="w2_raw", align_bytes=64)
+        w2_codes = keep.tile([P, H], I32, name="w2_codes", align_bytes=64)
+        w2_raw_scales = keep.tile([P, H], U8, name="w2_raw_scales", align_bytes=64)
+        w2_scales = keep.tile([P, H], U8, name="w2_scales", align_bytes=64)
+        w3_codes = keep.tile([P, H], I32, name="w3_codes", align_bytes=64)
+        w3_scales = keep.tile([P, H], U8, name="w3_scales", align_bytes=64)
+        nodes_in = keep.tile([P, NODE_BLOCKS, H], BF16, name="nodes_in")
+        b3_bc = keep.tile([P, H], BF16, name="b3_bc")
+        warm = keep.tile([P, 1], F32, name="warm")
+        count = keep.tile([P, NODE_BLOCKS], F32, name="count")
+        share = keep.tile([P, NODE_BLOCKS], F32, name="share")
+        idle_h2 = keep.tile([P, P, PACK], BF16, name="idle_h2", align_bytes=64)
+        idle_codes = keep.tile([P, P], I32, name="idle_codes", align_bytes=64)
+        idle_scales = keep.tile([P, P], U8, name="idle_scales", align_bytes=64)
+        b3_plus = keep.tile([P, H], F32, name="b3_plus")
+        base = [keep.tile([P, H], F32, name="base%d" % b) for b in range(NODE_BLOCKS)]
+        result = [keep.tile([P, H], F32, name="result%d" % b) for b in range(NODE_BLOCKS)]
+        acc = [psum.tile([P, H], F32, name="acc%d" % b) for b in range(NODE_BLOCKS)]
+
+        def load_bytes(block, j0, j1):
+            nc.sync.dma_start(
+                out=h1b[:, block, j0 * H : j1 * H],
+                in_=bytes_rows[block * P : (block + 1) * P, j0 * H : j1 * H],
+            )
+
+        nc.scalar.dma_start(out=mask_bf[:], in_=mask_attend.rearrange("b n j -> (b n) j").rearrange("(c p) j -> p c j", p=P))
+        nc.scalar.dma_start(out=k_scale[:], in_=h1_scale.rearrange("a b c (p t) -> p (a b c t)", t=PACK))
+        nc.scalar.dma_start(out=bias_bf[:], in_=b2.rearrange("(p t) -> p t", t=PACK))
+        nc.vector.memset(warm[:], 0.0)
+        nc.scalar.activation(out=warm[:], in_=warm[:], func=ACT.Relu)
+        nc.vector.memset(w2_raw_scales[:].bitcast(I32), 0)
+        nc.vector.memset(w3_scales[:].bitcast(I32), 0)
+        load_bytes(0, 0, 2)
+        load_bytes(0, 2, 4)
+        nc.sync.dma_start(out=w2_raw[:], in_=W2_words[0].rearrange("p n t -> p (n t)").bitcast(I32))
+        for q in range(4):
+            nc.sync.dma_start(
+                out=w2_raw_scales[32 * q : 32 * q + 4, :].bitcast(I32),
+                in_=W2_scales[0, 4 * q : 4 * q + 4, :].bitcast(I32),
+            )
+        for q in range(4):
+            nc.sync.dma_start(
+                out=w3_scales[32 * q : 32 * q + 4, :].bitcast(I32),
+                in_=W3_scales[0, 4 * q : 4 * q + 4, :].bitcast(I32),
+            )
+        load_bytes(0, 4, 12)
+        nc.sync.dma_start(out=w3_codes[:], in_=W3_words[0].rearrange("p n t -> p (n t)").bitcast(I32))
+        load_bytes(0, 12, 20)
+        load_bytes(0, 20, 28)
+        load_bytes(0, 28, 30)
+        for j in range(0, NEIGHBOURS, 8):
+            load_bytes(1, j, min(j + 8, NEIGHBOURS))
+        nc.sync.dma_start(out=nodes_in[:], in_=h_V.rearrange("b n h -> (b n) h").rearrange("(c p) h -> p c h", p=P))
+        nc.sync.dma_start(out=b3_bc[:], in_=b3.partition_broadcast(P))
+        make_identity(nc, ident[:])
+        nc.vector.tensor_copy(out=mask_f[:], in_=mask_bf[:].rearrange("p c j -> p (c j)"))
+
+        cast_tiles = {}
+        turned_tiles = {}
+        grouped1 = {}
+        codes1 = {}
+        first_out = {}
+        planes = {}
+        grouped2 = {}
+        codes2 = {}
+
+        def cast(i, m, on_scalar=False):
+            if i not in cast_tiles:
+                cast_tiles[i] = work.tile([P, UNIT, H], BF16, name="cast_tile", align_bytes=64, bufs=3)
+            g = i * UNIT + m
+            block, j = divmod(g, NEIGHBOURS)
+            src = h1b[:, block, j * H : (j + 1) * H].bitcast(FP8)
+            if on_scalar:
+                nc.scalar.activation(out=cast_tiles[i][:, m, :], in_=src, func=ACT.Copy, scale=mask_f[:, g : g + 1])
+            else:
+                nc.vector.tensor_scalar(
+                    out=cast_tiles[i][:, m, :], in0=src, scalar1=mask_f[:, g : g + 1], scalar2=None, op0=ALU.mult
+                )
+
+        def vector_casts(i, members):
+            for m in members:
+                if m not in CAST_ON_SCALAR:
+                    cast(i, m)
+
+        def turn(i, half):
+            bank = psum.tile([P, 2, 2 * P], F32, name="bank", bufs=2)
+            turned_tiles[i, half] = bank
+            for m in range(2):
+                words = cast_tiles[i][:, 2 * half + m, :].bitcast(F32)
+                for u in range(2):
+                    nc.tensor.transpose(bank[:, u, m * P : (m + 1) * P], words[:, u : 2 * P : 2], ident[:])
+
+        def scale_out(i, half):
+            if half == 0:
+                grouped1[i] = work.tile([P, TOK, PACK], BF16, name="grouped1", align_bytes=64)
+            bank = turned_tiles[i, half]
+            nc.vector.tensor_tensor(
+                out=grouped1[i][:, half * 2 * P : (half + 1) * 2 * P, :].rearrange("p n (u e) -> p n u e", e=2),
+                in0=bank[:].rearrange("p u n -> p (u n)").bitcast(BF16).rearrange("p (u n e) -> p n u e", u=2, e=2),
+                in1=k_scale[:].rearrange("p (u e) -> p u e", e=2).unsqueeze(1).to_broadcast([P, 2 * P, 2, 2]),
+                op=ALU.mult,
+            )
+
+        def quantize1(i):
+            c = work.tile([P, TOK], I32, name="c1", align_bytes=64)
+            s = work.tile([P, TOK], U8, name="s1", align_bytes=64)
+            nc.vector.quantize_mx(
+                out=c[:].bitcast(FP8X4), scales=s[:], in_=grouped1[i][:].rearrange("p n t -> p (n t)")
+            )
+            codes1[i] = (c, s)
+
+        def multiply1(i):
+            c, s = codes1[i]
+            for t in range(PACK):
+                bank = psum.tile([P, TOK], F32, name="bank1", bufs=4)
+                first_out[i, t] = bank
+                nc.tensor.matmul_mx(
+                    out=bank[:],
+                    lhsT=w2_codes[:, t * P : (t + 1) * P].bitcast(FP8X4),
+                    lhsT_scale=w2_scales[:, t * P : (t + 1) * P],
+                    rhs=c[:].bitcast(FP8X4),
+                    rhs_scale=s[:],
+                    start=True,
+                    stop=True,
+                )
+
+        def bias_relu(i, t, on_vector=False):
+            if i not in planes:
+                planes[i] = work.tile([P, 2, TOK, 2], BF16, name="plane_tile", align_bytes=64)
+            dst = planes[i][:, t // 2, :, t % 2]
+            if on_vector:
+                nc.vector.tensor_scalar(
+                    out=dst, in0=first_out[i, t][:], scalar1=bias_f[:, t : t + 1], scalar2=0.0, op0=ALU.add, op1=ALU.max
+                )
+            else:
+                nc.scalar.activation(out=dst, in_=first_out[i, t][:], func=ACT.Relu, bias=bias_f[:, t : t + 1])
+
+        def interleave(i, n0, n1, on_vector=False):
+            if i not in grouped2:
+                grouped2[i] = work.tile([P, TOK, PACK], BF16, name="grouped2", align_bytes=64)
+            dst = grouped2[i][:].rearrange("p n t -> p (n t)").bitcast(F32).rearrange("p (n u) -> p n u", u=2)
+            src = planes[i][:].rearrange("p u n e -> p (u n e)").bitcast(F32).rearrange("p (u n) -> p n u", u=2)
+            if on_vector:
+                nc.vector.tensor_copy(out=dst[:, n0:n1, :], in_=src[:, n0:n1, :])
+            else:
+                nc.scalar.copy(out=dst[:, n0:n1, :], in_=src[:, n0:n1, :])
+
+        def quantize2(i):
+            c = work.tile([P, TOK], I32, name="c2", align_bytes=64)
+            s = work.tile([P, TOK], U8, name="s2", align_bytes=64)
+            nc.vector.quantize_mx(
+                out=c[:].bitcast(FP8X4), scales=s[:], in_=grouped2[i][:].rearrange("p n t -> p (n t)")
+            )
+            codes2[i] = (c, s)
+
+        def multiply2(i):
+            c, s = codes2[i]
+            for m in range(UNIT):
+                block, j = divmod(i * UNIT + m, NEIGHBOURS)
+                nc.tensor.matmul_mx(
+                    out=acc[block][:],
+                    lhsT=c[:, m * P : (m + 1) * P].bitcast(FP8X4),
+                    lhsT_scale=s[:, m * P : (m + 1) * P],
+                    rhs=w3_codes[:].bitcast(FP8X4),
+                    rhs_scale=w3_scales[:],
+                    start=(j == 0),
+                    stop=(j == NEIGHBOURS - 1),
+                )
+
+        cast(0, 0)
+        cast(0, 1, on_scalar=True)
+        cast(0, 2)
+        cast(0, 3, on_scalar=True)
+        for m in CAST_ON_SCALAR:
+            cast(1, m, on_scalar=True)
+        turn(0, 0)
+        turn(0, 1)
+
+        last = UNITS - 1
+        for i in range(UNITS):
+            scale_out(i, 0)
+            if i == 0:
+                nc.vector.tensor_copy(
+                    out=w2_codes[:].rearrange("p (t m) -> p t m", t=PACK),
+                    in_=w2_raw[:].rearrange("p (m t) -> p t m", t=PACK),
+                )
+                nc.vector.tensor_copy(out=bias_f[:], in_=bias_bf[:])
+            if i >= 2:
+                quantize2(i - 2)
+                multiply2(i - 2)
+            if i < last:
+                vector_casts(i + 1, (0, 1))
+                turn(i + 1, 0)
+            scale_out(i, 1)
+            if i < last:
+                vector_casts(i + 1, (2, 3))
+                turn(i + 1, 1)
+            if i == 0:
+                nc.vector.tensor_copy(
+                    out=w2_scales[:].rearrange("p (t m) -> p m t", t=PACK),
+                    in_=w2_raw_scales[:].rearrange("p (m t) -> p m t", t=PACK),
+                )
+            quantize1(i)
+            if i == 1:
+                nc.vector.tensor_scalar(
+                    out=idle_h2[:],
+                    in0=bias_bf[:].unsqueeze(1).to_broadcast([P, P, PACK]),
+                    scalar1=0.0,
+                    scalar2=None,
+                    op0=ALU.max,
+                )
+                nc.vector.tensor_reduce(
+                    out=count[:], in_=mask_f[:].rearrange("p (c j) -> p c j", c=NODE_BLOCKS), op=ALU.add, axis=AXIS.X
+                )
+            if i == 2:
+                nc.vector.quantize_mx(
+                    out=idle_codes[:].bitcast(FP8X4),
+                    scales=idle_scales[:],
+                    in_=idle_h2[:].rearrange("p n t -> p (n t)"),
+                )
+                nc.vector.tensor_scalar(
+                    out=share[:], in0=count[:], scalar1=1.0 / NEIGHBOURS, scalar2=None, op0=ALU.mult
+                )
+            multiply1(i)
+            if i < last:
+                for t in range(PACK):
+                    bias_relu(i, t)
+                if i + 2 < UNITS:
+                    for m in CAST_ON_SCALAR:
+                        cast(i + 2, m, on_scalar=True)
+                interleave(i, 0, TOK)
+
+        idle_out = psum.tile([P, 2, 2 * P], F32, name="bank", bufs=2)
+        idle_row = idle_out[:].rearrange("p u n -> p (u n)")
+        nc.tensor.matmul_mx(
+            out=idle_row,
+            lhsT=idle_codes[:].bitcast(FP8X4),
+            lhsT_scale=idle_scales[:],
+            rhs=w3_codes[:].bitcast(FP8X4),
+            rhs_scale=w3_scales[:],
+            start=True,
+            stop=True,
+        )
+        bias_relu(last, 0)
+        bias_relu(last, 1)
+        bias_relu(last, 2, on_vector=True)
+        bias_relu(last, 3, on_vector=True)
+        quantize2(last - 1)
+        multiply2(last - 1)
+        interleave(last, 0, TOK // 2)
+        interleave(last, TOK // 2, TOK, on_vector=True)
+        nc.vector.tensor_tensor(out=b3_plus[:], in0=idle_row, in1=b3_bc[:], op=ALU.add)
+        quantize2(last)
+        multiply2(last)
+        for b in range(NODE_BLOCKS):
+            nc.vector.scalar_tensor_tensor(
+                out=base[b][:], in0=b3_plus[:], scalar=share[:, b : b + 1], in1=nodes_in[:, b, :], op0=ALU.mult, op1=ALU.add
+            )
+        for b in range(NODE_BLOCKS):
+            nc.vector.tensor_tensor(out=base[b][:], in0=base[b][:], in1=idle_row, op=ALU.subtract)
+        for b in range(NODE_BLOCKS):
+            nc.vector.scalar_tensor_tensor(
+                out=result[b][:], in0=acc[b][:], scalar=1.0 / NEIGHBOURS, in1=base[b][:], op0=ALU.mult, op1=ALU.add
+            )
+            nc.sync.dma_start(out=out_rows[b * P : (b + 1) * P, :], in_=result[b][:])

@@ -10,9 +10,9 @@ H = 512
 PACK = 4
 NODE_BLOCKS = NODES // P
 GROUPS = NODE_BLOCKS * NEIGHBOURS
-UNIT = 4
-UNITS = GROUPS // UNIT
-TOK = UNIT * P
+SIZES = [2] + [4] * 14 + [2]
+STARTS = [sum(SIZES[:i]) for i in range(len(SIZES))]
+UNITS = len(SIZES)
 FLOPS = 2 * (2 * NODES * NEIGHBOURS * H * H)
 
 F32 = mybir.dt.float32
@@ -25,7 +25,7 @@ ALU = mybir.AluOpType
 ACT = mybir.ActivationFunctionType
 AXIS = mybir.AxisListType
 
-CAST_ON_SCALAR = (3,)
+POOL_COLUMNS = 512
 
 
 def tile_mpnnlayer_pb_w8_kernel(
@@ -59,10 +59,11 @@ def tile_mpnnlayer_pb_w8_kernel(
         warm = keep.tile([P, 1], F32, name="warm")
         count = keep.tile([P, NODE_BLOCKS], F32, name="count")
         share = keep.tile([P, NODE_BLOCKS], F32, name="share")
+        masked_share = keep.tile([P, NODE_BLOCKS], F32, name="masked_share")
         idle_h2 = keep.tile([P, P, PACK], BF16, name="idle_h2", align_bytes=64)
         idle_codes = keep.tile([P, P], I32, name="idle_codes", align_bytes=64)
         idle_scales = keep.tile([P, P], U8, name="idle_scales", align_bytes=64)
-        b3_plus = keep.tile([P, H], F32, name="b3_plus")
+        idle_part = [keep.tile([P, H], F32, name="idle_part%d" % b) for b in range(NODE_BLOCKS)]
         base = [keep.tile([P, H], F32, name="base%d" % b) for b in range(NODE_BLOCKS)]
         result = [keep.tile([P, H], F32, name="result%d" % b) for b in range(NODE_BLOCKS)]
         acc = [psum.tile([P, H], F32, name="acc%d" % b) for b in range(NODE_BLOCKS)]
@@ -81,23 +82,22 @@ def tile_mpnnlayer_pb_w8_kernel(
         nc.vector.memset(w2_raw_scales[:].bitcast(I32), 0)
         nc.vector.memset(w3_scales[:].bitcast(I32), 0)
         load_bytes(0, 0, 2)
-        load_bytes(0, 2, 4)
+        load_bytes(0, 2, 6)
         nc.sync.dma_start(out=w2_raw[:], in_=W2_words[0].rearrange("p n t -> p (n t)").bitcast(I32))
         for q in range(4):
             nc.sync.dma_start(
                 out=w2_raw_scales[32 * q : 32 * q + 4, :].bitcast(I32),
                 in_=W2_scales[0, 4 * q : 4 * q + 4, :].bitcast(I32),
             )
+        load_bytes(0, 6, 14)
         for q in range(4):
             nc.sync.dma_start(
                 out=w3_scales[32 * q : 32 * q + 4, :].bitcast(I32),
                 in_=W3_scales[0, 4 * q : 4 * q + 4, :].bitcast(I32),
             )
-        load_bytes(0, 4, 12)
         nc.sync.dma_start(out=w3_codes[:], in_=W3_words[0].rearrange("p n t -> p (n t)").bitcast(I32))
-        load_bytes(0, 12, 20)
-        load_bytes(0, 20, 28)
-        load_bytes(0, 28, 30)
+        load_bytes(0, 14, 22)
+        load_bytes(0, 22, 30)
         for j in range(0, NEIGHBOURS, 8):
             load_bytes(1, j, min(j + 8, NEIGHBOURS))
         nc.sync.dma_start(out=nodes_in[:], in_=h_V.rearrange("b n h -> (b n) h").rearrange("(c p) h -> p c h", p=P))
@@ -116,8 +116,8 @@ def tile_mpnnlayer_pb_w8_kernel(
 
         def cast(i, m, on_scalar=False):
             if i not in cast_tiles:
-                cast_tiles[i] = work.tile([P, UNIT, H], BF16, name="cast_tile", align_bytes=64, bufs=3)
-            g = i * UNIT + m
+                cast_tiles[i] = work.tile([P, SIZES[i], H], BF16, name="cast_tile", align_bytes=64, bufs=4)
+            g = STARTS[i] + m
             block, j = divmod(g, NEIGHBOURS)
             src = h1b[:, block, j * H : (j + 1) * H].bitcast(FP8)
             if on_scalar:
@@ -127,12 +127,22 @@ def tile_mpnnlayer_pb_w8_kernel(
                     out=cast_tiles[i][:, m, :], in0=src, scalar1=mask_f[:, g : g + 1], scalar2=None, op0=ALU.mult
                 )
 
-        def vector_casts(i, members):
-            for m in members:
-                if m not in CAST_ON_SCALAR:
+        def on_vector(i):
+            return (0,) if i % 3 else (0, 1)
+
+        def vector_casts(i):
+            for m in range(SIZES[i]):
+                if m in on_vector(i):
                     cast(i, m)
 
+        def scalar_casts(i):
+            for m in range(SIZES[i]):
+                if m not in on_vector(i):
+                    cast(i, m, on_scalar=True)
+
         def turn(i, half):
+            if 2 * half >= SIZES[i]:
+                return
             bank = psum.tile([P, 2, 2 * P], F32, name="bank", bufs=2)
             turned_tiles[i, half] = bank
             for m in range(2):
@@ -141,8 +151,10 @@ def tile_mpnnlayer_pb_w8_kernel(
                     nc.tensor.transpose(bank[:, u, m * P : (m + 1) * P], words[:, u : 2 * P : 2], ident[:])
 
         def scale_out(i, half):
+            if 2 * half >= SIZES[i]:
+                return
             if half == 0:
-                grouped1[i] = work.tile([P, TOK, PACK], BF16, name="grouped1", align_bytes=64)
+                grouped1[i] = work.tile([P, SIZES[i] * P, PACK], BF16, name="grouped1", align_bytes=64)
             bank = turned_tiles[i, half]
             nc.vector.tensor_tensor(
                 out=grouped1[i][:, half * 2 * P : (half + 1) * 2 * P, :].rearrange("p n (u e) -> p n u e", e=2),
@@ -152,8 +164,8 @@ def tile_mpnnlayer_pb_w8_kernel(
             )
 
         def quantize1(i):
-            c = work.tile([P, TOK], I32, name="c1", align_bytes=64)
-            s = work.tile([P, TOK], U8, name="s1", align_bytes=64)
+            c = work.tile([P, SIZES[i] * P], I32, name="c1", align_bytes=64)
+            s = work.tile([P, SIZES[i] * P], U8, name="s1", align_bytes=64)
             nc.vector.quantize_mx(
                 out=c[:].bitcast(FP8X4), scales=s[:], in_=grouped1[i][:].rearrange("p n t -> p (n t)")
             )
@@ -162,7 +174,7 @@ def tile_mpnnlayer_pb_w8_kernel(
         def multiply1(i):
             c, s = codes1[i]
             for t in range(PACK):
-                bank = psum.tile([P, TOK], F32, name="bank1", bufs=4)
+                bank = psum.tile([P, SIZES[i] * P], F32, name="bank1", bufs=4)
                 first_out[i, t] = bank
                 nc.tensor.matmul_mx(
                     out=bank[:],
@@ -176,8 +188,8 @@ def tile_mpnnlayer_pb_w8_kernel(
 
         def bias_relu(i, t, on_vector=False):
             if i not in planes:
-                planes[i] = work.tile([P, 2, TOK, 2], BF16, name="plane_tile", align_bytes=64)
-            dst = planes[i][:, t // 2, :, t % 2]
+                planes[i] = work.tile([P, PACK, SIZES[i] * P], BF16, name="plane_tile", align_bytes=64)
+            dst = planes[i][:, t, :]
             if on_vector:
                 nc.vector.tensor_scalar(
                     out=dst, in0=first_out[i, t][:], scalar1=bias_f[:, t : t + 1], scalar2=0.0, op0=ALU.add, op1=ALU.max
@@ -185,19 +197,23 @@ def tile_mpnnlayer_pb_w8_kernel(
             else:
                 nc.scalar.activation(out=dst, in_=first_out[i, t][:], func=ACT.Relu, bias=bias_f[:, t : t + 1])
 
-        def interleave(i, n0, n1, on_vector=False):
+        def interleave(i, n0, n1, engine):
+            if n1 <= n0:
+                return
             if i not in grouped2:
-                grouped2[i] = work.tile([P, TOK, PACK], BF16, name="grouped2", align_bytes=64)
-            dst = grouped2[i][:].rearrange("p n t -> p (n t)").bitcast(F32).rearrange("p (n u) -> p n u", u=2)
-            src = planes[i][:].rearrange("p u n e -> p (u n e)").bitcast(F32).rearrange("p (u n) -> p n u", u=2)
-            if on_vector:
-                nc.vector.tensor_copy(out=dst[:, n0:n1, :], in_=src[:, n0:n1, :])
+                grouped2[i] = work.tile([P, SIZES[i] * P, PACK], BF16, name="grouped2", align_bytes=64)
+            dst = grouped2[i][:, n0:n1, :]
+            src = planes[i][:, :, n0:n1].rearrange("p t n -> p n t")
+            if engine == "vector":
+                nc.vector.tensor_copy(out=dst, in_=src)
+            elif engine == "scalar":
+                nc.scalar.copy(out=dst, in_=src)
             else:
-                nc.scalar.copy(out=dst[:, n0:n1, :], in_=src[:, n0:n1, :])
+                nc.gpsimd.tensor_scalar(out=dst, in0=src, scalar1=1.0, scalar2=0.0, op0=ALU.mult, op1=ALU.add)
 
         def quantize2(i):
-            c = work.tile([P, TOK], I32, name="c2", align_bytes=64)
-            s = work.tile([P, TOK], U8, name="s2", align_bytes=64)
+            c = work.tile([P, SIZES[i] * P], I32, name="c2", align_bytes=64)
+            s = work.tile([P, SIZES[i] * P], U8, name="s2", align_bytes=64)
             nc.vector.quantize_mx(
                 out=c[:].bitcast(FP8X4), scales=s[:], in_=grouped2[i][:].rearrange("p n t -> p (n t)")
             )
@@ -205,8 +221,8 @@ def tile_mpnnlayer_pb_w8_kernel(
 
         def multiply2(i):
             c, s = codes2[i]
-            for m in range(UNIT):
-                block, j = divmod(i * UNIT + m, NEIGHBOURS)
+            for m in range(SIZES[i]):
+                block, j = divmod(STARTS[i] + m, NEIGHBOURS)
                 nc.tensor.matmul_mx(
                     out=acc[block][:],
                     lhsT=c[:, m * P : (m + 1) * P].bitcast(FP8X4),
@@ -217,14 +233,11 @@ def tile_mpnnlayer_pb_w8_kernel(
                     stop=(j == NEIGHBOURS - 1),
                 )
 
-        cast(0, 0)
-        cast(0, 1, on_scalar=True)
-        cast(0, 2)
-        cast(0, 3, on_scalar=True)
-        for m in CAST_ON_SCALAR:
-            cast(1, m, on_scalar=True)
+        vector_casts(0)
+        scalar_casts(0)
+        scalar_casts(1)
         turn(0, 0)
-        turn(0, 1)
+        scalar_casts(2)
 
         last = UNITS - 1
         for i in range(UNITS):
@@ -235,16 +248,17 @@ def tile_mpnnlayer_pb_w8_kernel(
                     in_=w2_raw[:].rearrange("p (m t) -> p t m", t=PACK),
                 )
                 nc.vector.tensor_copy(out=bias_f[:], in_=bias_bf[:])
+            if i < last:
+                vector_casts(i + 1)
+                turn(i + 1, 0)
+            if i >= 2:
+                interleave(i - 2, POOL_COLUMNS * SIZES[i - 2] // 4, SIZES[i - 2] * P, "vector")
+            scale_out(i, 1)
+            if i < last:
+                turn(i + 1, 1)
             if i >= 2:
                 quantize2(i - 2)
                 multiply2(i - 2)
-            if i < last:
-                vector_casts(i + 1, (0, 1))
-                turn(i + 1, 0)
-            scale_out(i, 1)
-            if i < last:
-                vector_casts(i + 1, (2, 3))
-                turn(i + 1, 1)
             if i == 0:
                 nc.vector.tensor_copy(
                     out=w2_scales[:].rearrange("p (t m) -> p m t", t=PACK),
@@ -271,45 +285,59 @@ def tile_mpnnlayer_pb_w8_kernel(
                 nc.vector.tensor_scalar(
                     out=share[:], in0=count[:], scalar1=1.0 / NEIGHBOURS, scalar2=None, op0=ALU.mult
                 )
+                nc.vector.tensor_scalar(
+                    out=masked_share[:], in0=count[:], scalar1=1.0 / NEIGHBOURS, scalar2=-1.0, op0=ALU.mult, op1=ALU.add
+                )
             multiply1(i)
+            if i == 4:
+                nc.tensor.matmul_mx(
+                    out=acc[1][:],
+                    lhsT=idle_codes[:].bitcast(FP8X4),
+                    lhsT_scale=idle_scales[:],
+                    rhs=w3_codes[:].bitcast(FP8X4),
+                    rhs_scale=w3_scales[:],
+                    start=True,
+                    stop=True,
+                )
             if i < last:
                 for t in range(PACK):
                     bias_relu(i, t)
-                if i + 2 < UNITS:
-                    for m in CAST_ON_SCALAR:
-                        cast(i + 2, m, on_scalar=True)
-                interleave(i, 0, TOK)
+                if i + 3 < UNITS:
+                    scalar_casts(i + 3)
+            if i == 4:
+                for b in range(NODE_BLOCKS):
+                    nc.scalar.activation(
+                        out=idle_part[b][:], in_=acc[1][:], func=ACT.Copy, scale=masked_share[:, b : b + 1]
+                    )
+            if i < last - 1:
+                interleave(i, 0, POOL_COLUMNS * SIZES[i] // 4, "pool")
 
-        idle_out = psum.tile([P, 2, 2 * P], F32, name="bank", bufs=2)
-        idle_row = idle_out[:].rearrange("p u n -> p (u n)")
-        nc.tensor.matmul_mx(
-            out=idle_row,
-            lhsT=idle_codes[:].bitcast(FP8X4),
-            lhsT_scale=idle_scales[:],
-            rhs=w3_codes[:].bitcast(FP8X4),
-            rhs_scale=w3_scales[:],
-            start=True,
-            stop=True,
-        )
-        bias_relu(last, 0)
-        bias_relu(last, 1)
-        bias_relu(last, 2, on_vector=True)
-        bias_relu(last, 3, on_vector=True)
-        quantize2(last - 1)
-        multiply2(last - 1)
-        interleave(last, 0, TOK // 2)
-        interleave(last, TOK // 2, TOK, on_vector=True)
-        nc.vector.tensor_tensor(out=b3_plus[:], in0=idle_row, in1=b3_bc[:], op=ALU.add)
-        quantize2(last)
-        multiply2(last)
-        for b in range(NODE_BLOCKS):
-            nc.vector.scalar_tensor_tensor(
-                out=base[b][:], in0=b3_plus[:], scalar=share[:, b : b + 1], in1=nodes_in[:, b, :], op0=ALU.mult, op1=ALU.add
-            )
-        for b in range(NODE_BLOCKS):
-            nc.vector.tensor_tensor(out=base[b][:], in0=base[b][:], in1=idle_row, op=ALU.subtract)
-        for b in range(NODE_BLOCKS):
+            if i in (5, 6):
+                b = i - 5
+                nc.gpsimd.tensor_scalar(
+                    out=base[b][:], in0=b3_bc[:], scalar1=share[:, b : b + 1], scalar2=0.0, op0=ALU.mult, op1=ALU.add
+                )
+                nc.gpsimd.tensor_tensor(out=base[b][:], in0=base[b][:], in1=nodes_in[:, b, :], op=ALU.add)
+                nc.gpsimd.tensor_tensor(out=base[b][:], in0=base[b][:], in1=idle_part[b][:], op=ALU.add)
+
+        def finish(b):
             nc.vector.scalar_tensor_tensor(
                 out=result[b][:], in0=acc[b][:], scalar=1.0 / NEIGHBOURS, in1=base[b][:], op0=ALU.mult, op1=ALU.add
             )
             nc.sync.dma_start(out=out_rows[b * P : (b + 1) * P, :], in_=result[b][:])
+
+        finish(0)
+        bias_relu(last, 2, on_vector=True)
+        bias_relu(last, 3, on_vector=True)
+        interleave(last - 1, 0, 96, "pool")
+        interleave(last - 1, 96, 256, "scalar")
+        interleave(last - 1, 256, 512, "vector")
+        bias_relu(last, 0)
+        bias_relu(last, 1)
+        quantize2(last - 1)
+        multiply2(last - 1)
+        interleave(last, 0, 96, "scalar")
+        interleave(last, 96, 256, "vector")
+        quantize2(last)
+        multiply2(last)
+        finish(1)

@@ -25,7 +25,7 @@ ALU = mybir.AluOpType
 ACT = mybir.ActivationFunctionType
 AXIS = mybir.AxisListType
 
-POOL_COLUMNS = 512
+SCALAR_COLUMNS = {13: 384}
 
 
 def tile_mpnnlayer_pb_w8_kernel(
@@ -58,12 +58,14 @@ def tile_mpnnlayer_pb_w8_kernel(
         b3_bc = keep.tile([P, H], BF16, name="b3_bc")
         warm = keep.tile([P, 1], F32, name="warm")
         count = keep.tile([P, NODE_BLOCKS], F32, name="count")
-        share = keep.tile([P, NODE_BLOCKS], F32, name="share")
-        masked_share = keep.tile([P, NODE_BLOCKS], F32, name="masked_share")
+        minus_masked = keep.tile([P, NODE_BLOCKS], F32, name="minus_masked")
         idle_h2 = keep.tile([P, P, PACK], BF16, name="idle_h2", align_bytes=64)
         idle_codes = keep.tile([P, P], I32, name="idle_codes", align_bytes=64)
         idle_scales = keep.tile([P, P], U8, name="idle_scales", align_bytes=64)
-        idle_part = [keep.tile([P, H], F32, name="idle_part%d" % b) for b in range(NODE_BLOCKS)]
+        idle_row = keep.tile([P, H], F32, name="idle_row")
+        masked_diag = [keep.tile([P, P], F32, name="masked_diag%d" % b) for b in range(NODE_BLOCKS)]
+        thirty = keep.tile([P, P], BF16, name="thirty")
+        count_diag = [keep.tile([P, P], BF16, name="count_diag%d" % b) for b in range(NODE_BLOCKS)]
         base = [keep.tile([P, H], F32, name="base%d" % b) for b in range(NODE_BLOCKS)]
         result = [keep.tile([P, H], F32, name="result%d" % b) for b in range(NODE_BLOCKS)]
         acc = [psum.tile([P, H], F32, name="acc%d" % b) for b in range(NODE_BLOCKS)]
@@ -128,7 +130,7 @@ def tile_mpnnlayer_pb_w8_kernel(
                 )
 
         def on_vector(i):
-            return (0,) if i % 3 else (0, 1)
+            return (0, 1) if i == 0 else ()
 
         def vector_casts(i):
             for m in range(SIZES[i]):
@@ -202,14 +204,12 @@ def tile_mpnnlayer_pb_w8_kernel(
                 return
             if i not in grouped2:
                 grouped2[i] = work.tile([P, SIZES[i] * P, PACK], BF16, name="grouped2", align_bytes=64)
-            dst = grouped2[i][:, n0:n1, :]
-            src = planes[i][:, :, n0:n1].rearrange("p t n -> p n t")
+            dst = grouped2[i][:, n0:n1, :].rearrange("p (c i) t -> p c t i", i=4)
+            src = planes[i][:, :, n0:n1].rearrange("p t (c i) -> p c t i", i=4)
             if engine == "vector":
                 nc.vector.tensor_copy(out=dst, in_=src)
-            elif engine == "scalar":
-                nc.scalar.copy(out=dst, in_=src)
             else:
-                nc.gpsimd.tensor_scalar(out=dst, in0=src, scalar1=1.0, scalar2=0.0, op0=ALU.mult, op1=ALU.add)
+                nc.scalar.copy(out=dst, in_=src)
 
         def quantize2(i):
             c = work.tile([P, SIZES[i] * P], I32, name="c2", align_bytes=64)
@@ -252,7 +252,7 @@ def tile_mpnnlayer_pb_w8_kernel(
                 vector_casts(i + 1)
                 turn(i + 1, 0)
             if i >= 2:
-                interleave(i - 2, POOL_COLUMNS * SIZES[i - 2] // 4, SIZES[i - 2] * P, "vector")
+                interleave(i - 2, SCALAR_COLUMNS.get(i - 2, 0), SIZES[i - 2] * P, "vector")
             scale_out(i, 1)
             if i < last:
                 turn(i + 1, 1)
@@ -283,11 +283,24 @@ def tile_mpnnlayer_pb_w8_kernel(
                     in_=idle_h2[:].rearrange("p n t -> p (n t)"),
                 )
                 nc.vector.tensor_scalar(
-                    out=share[:], in0=count[:], scalar1=1.0 / NEIGHBOURS, scalar2=None, op0=ALU.mult
+                    out=minus_masked[:], in0=count[:], scalar1=float(NEIGHBOURS), scalar2=None, op0=ALU.subtract
                 )
-                nc.vector.tensor_scalar(
-                    out=masked_share[:], in0=count[:], scalar1=1.0 / NEIGHBOURS, scalar2=-1.0, op0=ALU.mult, op1=ALU.add
+            if i == 2:
+                nc.gpsimd.tensor_scalar(
+                    out=thirty[:], in0=ident[:], scalar1=float(NEIGHBOURS), scalar2=0.0, op0=ALU.mult, op1=ALU.add
                 )
+                for b in range(NODE_BLOCKS):
+                    nc.gpsimd.tensor_scalar(
+                        out=count_diag[b][:], in0=ident[:], scalar1=count[:, b : b + 1], scalar2=0.0, op0=ALU.mult, op1=ALU.add
+                    )
+                    nc.gpsimd.tensor_scalar(
+                        out=masked_diag[b][:],
+                        in0=ident[:],
+                        scalar1=minus_masked[:, b : b + 1],
+                        scalar2=0.0,
+                        op0=ALU.mult,
+                        op1=ALU.add,
+                    )
             multiply1(i)
             if i == 4:
                 nc.tensor.matmul_mx(
@@ -299,26 +312,22 @@ def tile_mpnnlayer_pb_w8_kernel(
                     start=True,
                     stop=True,
                 )
+            if i in (5, 6):
+                b = i - 5
+                nc.tensor.matmul(acc[1][:], lhsT=thirty[:], rhs=nodes_in[:, b, :], start=True, stop=False)
+                nc.tensor.matmul(acc[1][:], lhsT=count_diag[b][:], rhs=b3_bc[:], start=False, stop=False)
+                nc.tensor.matmul(acc[1][:], lhsT=masked_diag[b][:], rhs=idle_row[:], start=False, stop=True)
             if i < last:
-                for t in range(PACK):
+                for t in range(PACK if i < last - 1 else PACK - 1):
                     bias_relu(i, t)
                 if i + 3 < UNITS:
                     scalar_casts(i + 3)
             if i == 4:
-                for b in range(NODE_BLOCKS):
-                    nc.scalar.activation(
-                        out=idle_part[b][:], in_=acc[1][:], func=ACT.Copy, scale=masked_share[:, b : b + 1]
-                    )
-            if i < last - 1:
-                interleave(i, 0, POOL_COLUMNS * SIZES[i] // 4, "pool")
-
+                nc.scalar.copy(out=idle_row[:], in_=acc[1][:])
             if i in (5, 6):
-                b = i - 5
-                nc.gpsimd.tensor_scalar(
-                    out=base[b][:], in0=b3_bc[:], scalar1=share[:, b : b + 1], scalar2=0.0, op0=ALU.mult, op1=ALU.add
-                )
-                nc.gpsimd.tensor_tensor(out=base[b][:], in0=base[b][:], in1=nodes_in[:, b, :], op=ALU.add)
-                nc.gpsimd.tensor_tensor(out=base[b][:], in0=base[b][:], in1=idle_part[b][:], op=ALU.add)
+                nc.scalar.activation(out=base[i - 5][:], in_=acc[1][:], func=ACT.Copy, scale=1.0 / NEIGHBOURS)
+            if i < last - 1:
+                interleave(i, 0, SCALAR_COLUMNS.get(i, 0), "scalar")
 
         def finish(b):
             nc.vector.scalar_tensor_tensor(
@@ -326,18 +335,18 @@ def tile_mpnnlayer_pb_w8_kernel(
             )
             nc.sync.dma_start(out=out_rows[b * P : (b + 1) * P, :], in_=result[b][:])
 
-        finish(0)
-        bias_relu(last, 2, on_vector=True)
-        bias_relu(last, 3, on_vector=True)
-        interleave(last - 1, 0, 96, "pool")
-        interleave(last - 1, 96, 256, "scalar")
+        bias_relu(last - 1, 3, on_vector=True)
+        interleave(last - 1, 0, 256, "scalar")
         interleave(last - 1, 256, 512, "vector")
         bias_relu(last, 0)
         bias_relu(last, 1)
+        bias_relu(last, 2, on_vector=True)
+        bias_relu(last, 3, on_vector=True)
         quantize2(last - 1)
         multiply2(last - 1)
         interleave(last, 0, 96, "scalar")
         interleave(last, 96, 256, "vector")
         quantize2(last)
+        finish(0)
         multiply2(last)
         finish(1)

from contextlib import ExitStack

import concourse.mybir as mybir
from concourse.masks import make_identity

P = 128
NODES = 256
NEIGHBOURS = 30
H = 512
PACK = 4
NODE_BLOCKS = NODES // P
GROUPS = NODE_BLOCKS * NEIGHBOURS
SIZES = [2] + [4] * 14 + [2]
STARTS = [sum(SIZES[:i]) for i in range(len(SIZES))]
UNITS = len(SIZES)
FLOPS = 2 * (2 * NODES * NEIGHBOURS * H * H)

F32 = mybir.dt.float32
BF16 = mybir.dt.bfloat16
I32 = mybir.dt.int32
U8 = mybir.dt.uint8
FP8 = mybir.dt.float8_e4m3fn
FP8X4 = mybir.dt.float8_e4m3fn_x4
ALU = mybir.AluOpType
ACT = mybir.ActivationFunctionType
AXIS = mybir.AxisListType

SCALAR_COLUMNS = {13: 384}


def tile_mpnnlayer_pb_w8_kernel(
    tc, h1_bytes, h1_scale, h_V, mask_attend, W2_words, W2_scales, b2, W3_words, W3_scales, b3, out
):
    nc = tc.nc
    bytes_rows = h1_bytes.rearrange("b n j k -> (b n) (j k)")
    out_rows = out.rearrange("b n h -> (b n) h")

    with ExitStack() as ctx:
        ctx.enter_context(tc.manual_schedule())
        keep = ctx.enter_context(tc.tile_pool(name="keep", bufs=1))
        work = ctx.enter_context(tc.tile_pool(name="work", bufs=2))
        psum = ctx.enter_context(tc.psum_pool(name="psum", bufs=1))

        h1b = keep.tile([P, NODE_BLOCKS, NEIGHBOURS * H], U8, name="h1b", align_bytes=64)
        mask_bf = keep.tile([P, NODE_BLOCKS, NEIGHBOURS], BF16, name="mask_bf")
        mask_f = keep.tile([P, GROUPS], F32, name="mask_f")
        k_scale = keep.tile([P, PACK], F32, name="k_scale")
        bias_bf = keep.tile([P, PACK], BF16, name="bias_bf")
        bias_f = keep.tile([P, PACK], F32, name="bias_f")
        ident = keep.tile([P, P], F32, name="ident")
        w2_raw = keep.tile([P, H], I32, name="w2_raw", align_bytes=64)
        w2_codes = keep.tile([P, H], I32, name="w2_codes", align_bytes=64)
        w2_raw_scales = keep.tile([P, H], U8, name="w2_raw_scales", align_bytes=64)
        w2_scales = keep.tile([P, H], U8, name="w2_scales", align_bytes=64)
        w3_codes = keep.tile([P, H], I32, name="w3_codes", align_bytes=64)
        w3_scales = keep.tile([P, H], U8, name="w3_scales", align_bytes=64)
        nodes_in = keep.tile([P, NODE_BLOCKS, H], BF16, name="nodes_in")
        b3_bc = keep.tile([P, H], BF16, name="b3_bc")
        warm = keep.tile([P, 1], F32, name="warm")
        count = keep.tile([P, NODE_BLOCKS], F32, name="count")
        minus_masked = keep.tile([P, NODE_BLOCKS], F32, name="minus_masked")
        idle_h2 = keep.tile([P, P, PACK], BF16, name="idle_h2", align_bytes=64)
        idle_codes = keep.tile([P, P], I32, name="idle_codes", align_bytes=64)
        idle_scales = keep.tile([P, P], U8, name="idle_scales", align_bytes=64)
        idle_row = keep.tile([P, H], F32, name="idle_row")
        masked_diag = [keep.tile([P, P], F32, name="masked_diag%d" % b) for b in range(NODE_BLOCKS)]
        thirty = keep.tile([P, P], BF16, name="thirty")
        count_diag = [keep.tile([P, P], BF16, name="count_diag%d" % b) for b in range(NODE_BLOCKS)]
        base = [keep.tile([P, H], F32, name="base%d" % b) for b in range(NODE_BLOCKS)]
        result = [keep.tile([P, H], F32, name="result%d" % b) for b in range(NODE_BLOCKS)]
        acc = [psum.tile([P, H], F32, name="acc%d" % b) for b in range(NODE_BLOCKS)]

        def load_bytes(block, j0, j1):
            nc.sync.dma_start(
                out=h1b[:, block, j0 * H : j1 * H],
                in_=bytes_rows[block * P : (block + 1) * P, j0 * H : j1 * H],
            )

        nc.scalar.dma_start(out=mask_bf[:], in_=mask_attend.rearrange("b n j -> (b n) j").rearrange("(c p) j -> p c j", p=P))
        nc.scalar.dma_start(out=k_scale[:], in_=h1_scale.rearrange("a b c (p t) -> p (a b c t)", t=PACK))
        nc.scalar.dma_start(out=bias_bf[:], in_=b2.rearrange("(p t) -> p t", t=PACK))
        nc.vector.memset(warm[:], 0.0)
        nc.scalar.activation(out=warm[:], in_=warm[:], func=ACT.Relu)
        nc.vector.memset(w2_raw_scales[:].bitcast(I32), 0)
        nc.vector.memset(w3_scales[:].bitcast(I32), 0)
        load_bytes(0, 0, 2)
        load_bytes(0, 2, 6)
        nc.sync.dma_start(out=w2_raw[:], in_=W2_words[0].rearrange("p n t -> p (n t)").bitcast(I32))
        for q in range(4):
            nc.sync.dma_start(
                out=w2_raw_scales[32 * q : 32 * q + 4, :].bitcast(I32),
                in_=W2_scales[0, 4 * q : 4 * q + 4, :].bitcast(I32),
            )
        load_bytes(0, 6, 14)
        for q in range(4):
            nc.sync.dma_start(
                out=w3_scales[32 * q : 32 * q + 4, :].bitcast(I32),
                in_=W3_scales[0, 4 * q : 4 * q + 4, :].bitcast(I32),
            )
        nc.sync.dma_start(out=w3_codes[:], in_=W3_words[0].rearrange("p n t -> p (n t)").bitcast(I32))
        load_bytes(0, 14, 22)
        load_bytes(0, 22, 30)
        for j in range(0, NEIGHBOURS, 8):
            load_bytes(1, j, min(j + 8, NEIGHBOURS))
        nc.sync.dma_start(out=nodes_in[:], in_=h_V.rearrange("b n h -> (b n) h").rearrange("(c p) h -> p c h", p=P))
        nc.sync.dma_start(out=b3_bc[:], in_=b3.partition_broadcast(P))
        make_identity(nc, ident[:])
        nc.vector.tensor_copy(out=mask_f[:], in_=mask_bf[:].rearrange("p c j -> p (c j)"))

        cast_tiles = {}
        turned_tiles = {}
        grouped1 = {}
        codes1 = {}
        first_out = {}
        planes = {}
        grouped2 = {}
        codes2 = {}

        def cast(i, m, on_scalar=False):
            if i not in cast_tiles:
                cast_tiles[i] = work.tile([P, SIZES[i], H], BF16, name="cast_tile", align_bytes=64, bufs=4)
            g = STARTS[i] + m
            block, j = divmod(g, NEIGHBOURS)
            src = h1b[:, block, j * H : (j + 1) * H].bitcast(FP8)
            if on_scalar:
                nc.scalar.activation(out=cast_tiles[i][:, m, :], in_=src, func=ACT.Copy, scale=mask_f[:, g : g + 1])
            else:
                nc.vector.tensor_scalar(
                    out=cast_tiles[i][:, m, :], in0=src, scalar1=mask_f[:, g : g + 1], scalar2=None, op0=ALU.mult
                )

        def on_vector(i):
            return (0, 1) if i == 0 else ()

        def vector_casts(i):
            for m in range(SIZES[i]):
                if m in on_vector(i):
                    cast(i, m)

        def scalar_casts(i):
            for m in range(SIZES[i]):
                if m not in on_vector(i):
                    cast(i, m, on_scalar=True)

        def turn(i, half):
            if 2 * half >= SIZES[i]:
                return
            bank = psum.tile([P, 2, 2 * P], F32, name="bank", bufs=2)
            turned_tiles[i, half] = bank
            for m in range(2):
                words = cast_tiles[i][:, 2 * half + m, :].bitcast(F32)
                for u in range(2):
                    nc.tensor.transpose(bank[:, u, m * P : (m + 1) * P], words[:, u : 2 * P : 2], ident[:])

        def scale_out(i, half):
            if 2 * half >= SIZES[i]:
                return
            if half == 0:
                grouped1[i] = work.tile([P, SIZES[i] * P, PACK], BF16, name="grouped1", align_bytes=64)
            bank = turned_tiles[i, half]
            nc.vector.tensor_tensor(
                out=grouped1[i][:, half * 2 * P : (half + 1) * 2 * P, :].rearrange("p n (u e) -> p n u e", e=2),
                in0=bank[:].rearrange("p u n -> p (u n)").bitcast(BF16).rearrange("p (u n e) -> p n u e", u=2, e=2),
                in1=k_scale[:].rearrange("p (u e) -> p u e", e=2).unsqueeze(1).to_broadcast([P, 2 * P, 2, 2]),
                op=ALU.mult,
            )

        def quantize1(i):
            c = work.tile([P, SIZES[i] * P], I32, name="c1", align_bytes=64)
            s = work.tile([P, SIZES[i] * P], U8, name="s1", align_bytes=64)
            nc.vector.quantize_mx(
                out=c[:].bitcast(FP8X4), scales=s[:], in_=grouped1[i][:].rearrange("p n t -> p (n t)")
            )
            codes1[i] = (c, s)

        def multiply1(i):
            c, s = codes1[i]
            for t in range(PACK):
                bank = psum.tile([P, SIZES[i] * P], F32, name="bank1", bufs=4)
                first_out[i, t] = bank
                nc.tensor.matmul_mx(
                    out=bank[:],
                    lhsT=w2_codes[:, t * P : (t + 1) * P].bitcast(FP8X4),
                    lhsT_scale=w2_scales[:, t * P : (t + 1) * P],
                    rhs=c[:].bitcast(FP8X4),
                    rhs_scale=s[:],
                    start=True,
                    stop=True,
                )

        def bias_relu(i, t, on_vector=False):
            if i not in planes:
                planes[i] = work.tile([P, PACK, SIZES[i] * P], BF16, name="plane_tile", align_bytes=64)
            dst = planes[i][:, t, :]
            if on_vector:
                nc.vector.tensor_scalar(
                    out=dst, in0=first_out[i, t][:], scalar1=bias_f[:, t : t + 1], scalar2=0.0, op0=ALU.add, op1=ALU.max
                )
            else:
                nc.scalar.activation(out=dst, in_=first_out[i, t][:], func=ACT.Relu, bias=bias_f[:, t : t + 1])

        def interleave(i, n0, n1, engine):
            if n1 <= n0:
                return
            if i not in grouped2:
                grouped2[i] = work.tile([P, SIZES[i] * P, PACK], BF16, name="grouped2", align_bytes=64)
            dst = grouped2[i][:, n0:n1, :].rearrange("p (c i) t -> p c t i", i=4)
            src = planes[i][:, :, n0:n1].rearrange("p t (c i) -> p c t i", i=4)
            if engine == "vector":
                nc.vector.tensor_copy(out=dst, in_=src)
            else:
                nc.scalar.copy(out=dst, in_=src)

        def quantize2(i):
            c = work.tile([P, SIZES[i] * P], I32, name="c2", align_bytes=64)
            s = work.tile([P, SIZES[i] * P], U8, name="s2", align_bytes=64)
            nc.vector.quantize_mx(
                out=c[:].bitcast(FP8X4), scales=s[:], in_=grouped2[i][:].rearrange("p n t -> p (n t)")
            )
            codes2[i] = (c, s)

        def multiply2(i):
            c, s = codes2[i]
            for m in range(SIZES[i]):
                block, j = divmod(STARTS[i] + m, NEIGHBOURS)
                nc.tensor.matmul_mx(
                    out=acc[block][:],
                    lhsT=c[:, m * P : (m + 1) * P].bitcast(FP8X4),
                    lhsT_scale=s[:, m * P : (m + 1) * P],
                    rhs=w3_codes[:].bitcast(FP8X4),
                    rhs_scale=w3_scales[:],
                    start=(j == 0),
                    stop=(j == NEIGHBOURS - 1),
                )

        vector_casts(0)
        scalar_casts(0)
        scalar_casts(1)
        turn(0, 0)
        scalar_casts(2)

        last = UNITS - 1
        for i in range(UNITS):
            scale_out(i, 0)
            if i == 0:
                nc.vector.tensor_copy(
                    out=w2_codes[:].rearrange("p (t m) -> p t m", t=PACK),
                    in_=w2_raw[:].rearrange("p (m t) -> p t m", t=PACK),
                )
                nc.vector.tensor_copy(out=bias_f[:], in_=bias_bf[:])
            if i < last:
                vector_casts(i + 1)
                turn(i + 1, 0)
            if i >= 2:
                interleave(i - 2, SCALAR_COLUMNS.get(i - 2, 0), SIZES[i - 2] * P, "vector")
            scale_out(i, 1)
            if i < last:
                turn(i + 1, 1)
            if i >= 2:
                quantize2(i - 2)
                multiply2(i - 2)
            if i == 0:
                nc.vector.tensor_copy(
                    out=w2_scales[:].rearrange("p (t m) -> p m t", t=PACK),
                    in_=w2_raw_scales[:].rearrange("p (m t) -> p m t", t=PACK),
                )
            quantize1(i)
            if i == 1:
                nc.vector.tensor_scalar(
                    out=idle_h2[:],
                    in0=bias_bf[:].unsqueeze(1).to_broadcast([P, P, PACK]),
                    scalar1=0.0,
                    scalar2=None,
                    op0=ALU.max,
                )
                nc.vector.tensor_reduce(
                    out=count[:], in_=mask_f[:].rearrange("p (c j) -> p c j", c=NODE_BLOCKS), op=ALU.add, axis=AXIS.X
                )
            if i == 2:
                nc.vector.quantize_mx(
                    out=idle_codes[:].bitcast(FP8X4),
                    scales=idle_scales[:],
                    in_=idle_h2[:].rearrange("p n t -> p (n t)"),
                )
                nc.vector.tensor_scalar(
                    out=minus_masked[:], in0=count[:], scalar1=float(NEIGHBOURS), scalar2=None, op0=ALU.subtract
                )
            if i == 2:
                nc.gpsimd.tensor_scalar(
                    out=thirty[:], in0=ident[:], scalar1=float(NEIGHBOURS), scalar2=0.0, op0=ALU.mult, op1=ALU.add
                )
                for b in range(NODE_BLOCKS):
                    nc.gpsimd.tensor_scalar(
                        out=count_diag[b][:], in0=ident[:], scalar1=count[:, b : b + 1], scalar2=0.0, op0=ALU.mult, op1=ALU.add
                    )
                    nc.gpsimd.tensor_scalar(
                        out=masked_diag[b][:],
                        in0=ident[:],
                        scalar1=minus_masked[:, b : b + 1],
                        scalar2=0.0,
                        op0=ALU.mult,
                        op1=ALU.add,
                    )
            multiply1(i)
            if i == 4:
                nc.tensor.matmul_mx(
                    out=acc[1][:],
                    lhsT=idle_codes[:].bitcast(FP8X4),
                    lhsT_scale=idle_scales[:],
                    rhs=w3_codes[:].bitcast(FP8X4),
                    rhs_scale=w3_scales[:],
                    start=True,
                    stop=True,
                )
            if i in (5, 6):
                b = i - 5
                nc.tensor.matmul(acc[1][:], lhsT=thirty[:], rhs=nodes_in[:, b, :], start=True, stop=False)
                nc.tensor.matmul(acc[1][:], lhsT=count_diag[b][:], rhs=b3_bc[:], start=False, stop=False)
                nc.tensor.matmul(acc[1][:], lhsT=masked_diag[b][:], rhs=idle_row[:], start=False, stop=True)
            if i < last:
                for t in range(PACK if i < last - 1 else PACK - 1):
                    bias_relu(i, t)
                if i + 3 < UNITS:
                    scalar_casts(i + 3)
            if i == 4:
                nc.scalar.copy(out=idle_row[:], in_=acc[1][:])
            if i in (5, 6):
                nc.scalar.activation(out=base[i - 5][:], in_=acc[1][:], func=ACT.Copy, scale=1.0 / NEIGHBOURS)
            if i < last - 1:
                interleave(i, 0, SCALAR_COLUMNS.get(i, 0), "scalar")

        def finish(b):
            nc.vector.scalar_tensor_tensor(
                out=result[b][:], in0=acc[b][:], scalar=1.0 / NEIGHBOURS, in1=base[b][:], op0=ALU.mult, op1=ALU.add
            )
            nc.sync.dma_start(out=out_rows[b * P : (b + 1) * P, :], in_=result[b][:])

        bias_relu(last - 1, 3, on_vector=True)
        interleave(last - 1, 0, 256, "scalar")
        interleave(last - 1, 256, 512, "vector")
        bias_relu(last, 0)
        bias_relu(last, 1)
        bias_relu(last, 2, on_vector=True)
        bias_relu(last, 3, on_vector=True)
        quantize2(last - 1)
        multiply2(last - 1)
        interleave(last, 0, 96, "scalar")
        interleave(last, 96, 256, "vector")
        quantize2(last)
        finish(0)
        multiply2(last)
        finish(1)
